import numpy as np
import ml_dtypes

BF16 = ml_dtypes.bfloat16


def bf(x):
    return np.asarray(x, np.float32).astype(BF16)


def f32(x):
    return np.asarray(x, np.float32)


def f64(x):
    return np.asarray(x).astype(np.float64)


def striped(idx):
    return np.tile(idx.reshape(-1, 16).T, (8, 1))


S, D, M, R, Q, N = 1024, 128, 512, 64, 4, 256


def setup_inputs():
    return {"table": bf(np.random.standard_normal((S, D))), "w": bf(np.random.standard_normal((D, M)) / np.sqrt(D)), "b": f32(0.1 * np.random.standard_normal((M, 1))), "offs": striped(np.random.permutation(S)[:N])}


def reference(table, w, b, offs):
    idx = offs[:16].T.reshape(-1)
    h = np.maximum(f64(w).T @ f64(table)[idx].T + f64(b), 0.0)
    return h.reshape(M, R, Q).max(axis=2)

@@ -1,0 +1,67 @@
+import concourse.mybir as mybir
+from concourse.masks import make_identity
+
+BF16, F32, U16 = mybir.dt.bfloat16, mybir.dt.float32, mybir.dt.uint16
+ADD, MAX = mybir.AluOpType.add, mybir.AluOpType.max
+
+P = 128
+S, D = 1024, 128
+M = 512
+N, Q = 256, 4
+R = N // Q
+POINT_BLOCKS = S // P
+FEATURE_BLOCKS = M // P
+
+FLOPS = 2 * D * M * N
+
+
+def tile_cls_model_kernel(tc, table, w, b, offs, out):
+    nc = tc.nc
+    with (
+        tc.tile_pool(name="held", bufs=1) as held,
+        tc.tile_pool(name="work", bufs=2) as work,
+        tc.psum_pool(name="flip", bufs=4) as flip,
+        tc.psum_pool(name="prod", bufs=4) as prod,
+    ):
+        offsets = held.tile([P, N // 16], U16, name="offsets")
+        nc.sync.dma_start(offsets[:], offs)
+
+        rows = held.tile([P, POINT_BLOCKS, D], BF16, name="rows")
+        nc.sync.dma_start(rows[:], table.rearrange("(c p) d -> p c d", p=P))
+
+        weights = held.tile([D, M], BF16, name="weights")
+        nc.scalar.dma_start(weights[:], w)
+
+        bias = held.tile([P, FEATURE_BLOCKS], F32, name="bias")
+        with nc.allow_non_contiguous_dma(reason="one float32 of the bias to a partition"):
+            nc.scalar.dma_start(bias[:], b.rearrange("(k p) one -> p (k one)", p=P))
+
+        identity = held.tile([P, P], BF16, name="identity")
+        make_identity(nc, identity[:])
+
+        points = held.tile([D, S], BF16, name="points")
+        for c in range(POINT_BLOCKS):
+            flipped = flip.tile([D, P], BF16, name="flipped")
+            nc.tensor.transpose(flipped[:], rows[:, c, :], identity[:])
+            nc.vector.tensor_copy(points[:, c * P : (c + 1) * P], flipped[:])
+
+        pooled = held.tile([P, FEATURE_BLOCKS, R], F32, name="pooled")
+        for k in range(FEATURE_BLOCKS):
+            product = prod.tile([P, N], F32, name="product")
+            nc.tensor.matmul(
+                product[:],
+                weights[:, k * P : (k + 1) * P],
+                points[:].indirect(offsets[:]),
+                start=True,
+                stop=True,
+            )
+            peak = work.tile([P, R], F32, name="peak")
+            nc.vector.tensor_reduce(
+                out=peak[:],
+                in_=product[:].rearrange("p (r q) -> p r q", q=Q),
+                axis=mybir.AxisListType.X,
+                op=MAX,
+            )
+            nc.vector.tensor_scalar(pooled[:, k, :], peak[:], bias[:, k : k + 1], 0.0, op0=ADD, op1=MAX)
+
+        nc.sync.dma_start(out.rearrange("(k p) r -> p k r", p=P), pooled[:])

@@ -9,7 +9,8 @@ S, D = 1024, 128
 M = 512
 N, Q = 256, 4
 R = N // Q
-POINT_BLOCKS = S // P
+CHUNK = 2 * P
+CHUNKS = S // CHUNK
 FEATURE_BLOCKS = M // P
 
 FLOPS = 2 * D * M * N
@@ -20,17 +21,21 @@ def tile_cls_model_kernel(tc, table, w, b, offs, out):
     with (
         tc.tile_pool(name="held", bufs=1) as held,
         tc.tile_pool(name="work", bufs=2) as work,
-        tc.psum_pool(name="flip", bufs=4) as flip,
-        tc.psum_pool(name="prod", bufs=4) as prod,
+        tc.psum_pool(name="flip", bufs=CHUNKS) as flip,
+        tc.psum_pool(name="prod", bufs=FEATURE_BLOCKS) as prod,
     ):
+        chunked = table.rearrange("(c e p) d -> c p e d", e=CHUNK // P, p=P)
+        rows = []
+        for c in range(CHUNKS):
+            rows.append(held.tile([P, CHUNK // P, D], BF16, name=f"rows{c}"))
+            queue = nc.sync if c % 2 == 0 else nc.scalar
+            queue.dma_start(rows[c][:], chunked[c])
+
         offsets = held.tile([P, N // 16], U16, name="offsets")
         nc.sync.dma_start(offsets[:], offs)
 
-        rows = held.tile([P, POINT_BLOCKS, D], BF16, name="rows")
-        nc.sync.dma_start(rows[:], table.rearrange("(c p) d -> p c d", p=P))
-
         weights = held.tile([D, M], BF16, name="weights")
-        nc.scalar.dma_start(weights[:], w)
+        nc.sync.dma_start(weights[:], w)
 
         bias = held.tile([P, FEATURE_BLOCKS], F32, name="bias")
         with nc.allow_non_contiguous_dma(reason="one float32 of the bias to a partition"):
@@ -40,10 +45,11 @@ def tile_cls_model_kernel(tc, table, w, b, offs, out):
         make_identity(nc, identity[:])
 
         points = held.tile([D, S], BF16, name="points")
-        for c in range(POINT_BLOCKS):
-            flipped = flip.tile([D, P], BF16, name="flipped")
-            nc.tensor.transpose(flipped[:], rows[:, c, :], identity[:])
-            nc.vector.tensor_copy(points[:, c * P : (c + 1) * P], flipped[:])
+        for c in range(CHUNKS):
+            flipped = flip.tile([D, CHUNK], BF16, name="flipped")
+            for e in range(CHUNK // P):
+                nc.tensor.transpose(flipped[:, e * P : (e + 1) * P], rows[c][:, e, :], identity[:])
+            nc.vector.tensor_copy(points[:, c * CHUNK : (c + 1) * CHUNK], flipped[:])
 
         pooled = held.tile([P, FEATURE_BLOCKS, R], F32, name="pooled")
         for k in range(FEATURE_BLOCKS):

@@ -12,6 +12,8 @@ R = N // Q
 CHUNK = 2 * P
 CHUNKS = S // CHUNK
 FEATURE_BLOCKS = M // P
+BANK = 512
+WARM_UPS = 6
 
 FLOPS = 2 * D * M * N
 
@@ -21,7 +23,8 @@ def tile_cls_model_kernel(tc, table, w, b, offs, out):
     with (
         tc.tile_pool(name="held", bufs=1) as held,
         tc.tile_pool(name="work", bufs=2) as work,
-        tc.psum_pool(name="flip", bufs=CHUNKS) as flip,
+        tc.psum_pool(name="idle", bufs=1) as idle,
+        tc.psum_pool(name="flip", bufs=CHUNKS - 1) as flip,
         tc.psum_pool(name="prod", bufs=FEATURE_BLOCKS) as prod,
     ):
         chunked = table.rearrange("(c e p) d -> c p e d", e=CHUNK // P, p=P)
@@ -43,6 +46,12 @@ def tile_cls_model_kernel(tc, table, w, b, offs, out):
 
         identity = held.tile([P, P], BF16, name="identity")
         make_identity(nc, identity[:])
+
+        zeros = held.tile([P, BANK], BF16, name="zeros")
+        nc.vector.memset(zeros[:], 0.0)
+        unused = idle.tile([P, BANK], F32, name="unused")
+        for turn in range(WARM_UPS):
+            nc.tensor.matmul(unused[:], zeros[:, 0:P], zeros[:], start=True, stop=True)
 
         points = held.tile([D, S], BF16, name="points")
         for c in range(CHUNKS):

@@ -12,8 +12,6 @@ R = N // Q
 CHUNK = 2 * P
 CHUNKS = S // CHUNK
 FEATURE_BLOCKS = M // P
-BANK = 512
-WARM_UPS = 6
 
 FLOPS = 2 * D * M * N
 
@@ -22,9 +20,8 @@ def tile_cls_model_kernel(tc, table, w, b, offs, out):
     nc = tc.nc
     with (
         tc.tile_pool(name="held", bufs=1) as held,
-        tc.tile_pool(name="work", bufs=2) as work,
-        tc.psum_pool(name="idle", bufs=1) as idle,
-        tc.psum_pool(name="flip", bufs=CHUNKS - 1) as flip,
+        tc.tile_pool(name="work", bufs=FEATURE_BLOCKS) as work,
+        tc.psum_pool(name="flip", bufs=CHUNKS) as flip,
         tc.psum_pool(name="prod", bufs=FEATURE_BLOCKS) as prod,
     ):
         chunked = table.rearrange("(c e p) d -> c p e d", e=CHUNK // P, p=P)
@@ -47,12 +44,6 @@ def tile_cls_model_kernel(tc, table, w, b, offs, out):
         identity = held.tile([P, P], BF16, name="identity")
         make_identity(nc, identity[:])
 
-        zeros = held.tile([P, BANK], BF16, name="zeros")
-        nc.vector.memset(zeros[:], 0.0)
-        unused = idle.tile([P, BANK], F32, name="unused")
-        for turn in range(WARM_UPS):
-            nc.tensor.matmul(unused[:], zeros[:, 0:P], zeros[:], start=True, stop=True)
-
         points = held.tile([D, S], BF16, name="points")
         for c in range(CHUNKS):
             flipped = flip.tile([D, CHUNK], BF16, name="flipped")
@@ -60,7 +51,6 @@ def tile_cls_model_kernel(tc, table, w, b, offs, out):
                 nc.tensor.transpose(flipped[:, e * P : (e + 1) * P], rows[c][:, e, :], identity[:])
             nc.vector.tensor_copy(points[:, c * CHUNK : (c + 1) * CHUNK], flipped[:])
 
-        pooled = held.tile([P, FEATURE_BLOCKS, R], F32, name="pooled")
         for k in range(FEATURE_BLOCKS):
             product = prod.tile([P, N], F32, name="product")
             nc.tensor.matmul(
@@ -77,6 +67,7 @@ def tile_cls_model_kernel(tc, table, w, b, offs, out):
                 axis=mybir.AxisListType.X,
                 op=MAX,
             )
-            nc.vector.tensor_scalar(pooled[:, k, :], peak[:], bias[:, k : k + 1], 0.0, op0=ADD, op1=MAX)
-
-        nc.sync.dma_start(out.rearrange("(k p) r -> p k r", p=P), pooled[:])
+            pooled = work.tile([P, R], F32, name="pooled")
+            nc.vector.tensor_scalar(pooled[:], peak[:], bias[:, k : k + 1], 0.0, op0=ADD, op1=MAX)
+            queue = nc.sync if k % 2 == 0 else nc.scalar
+            queue.dma_start(out[k * P : (k + 1) * P, :], pooled[:])

@@ -24,7 +24,7 @@ def tile_cls_model_kernel(tc, table, w, b, offs, out):
         tc.psum_pool(name="flip", bufs=CHUNKS) as flip,
         tc.psum_pool(name="prod", bufs=FEATURE_BLOCKS) as prod,
     ):
-        chunked = table.rearrange("(c e p) d -> c p e d", e=CHUNK // P, p=P)
+        chunked = table.rearrange("(c p e) d -> c p e d", p=P, e=CHUNK // P)
         rows = []
         for c in range(CHUNKS):
             rows.append(held.tile([P, CHUNK // P, D], BF16, name=f"rows{c}"))
@@ -49,7 +49,10 @@ def tile_cls_model_kernel(tc, table, w, b, offs, out):
             flipped = flip.tile([D, CHUNK], BF16, name="flipped")
             for e in range(CHUNK // P):
                 nc.tensor.transpose(flipped[:, e * P : (e + 1) * P], rows[c][:, e, :], identity[:])
-            nc.vector.tensor_copy(points[:, c * CHUNK : (c + 1) * CHUNK], flipped[:])
+            nc.vector.tensor_copy(
+                points[:, c * CHUNK : (c + 1) * CHUNK].rearrange("d (p e) -> d p e", p=P),
+                flipped[:].rearrange("d (e p) -> d p e", p=P),
+            )
 
         for k in range(FEATURE_BLOCKS):
             product = prod.tile([P, N], F32, name="product")

@@ -3,6 +3,7 @@ from concourse.masks import make_identity
 
 BF16, F32, U16 = mybir.dt.bfloat16, mybir.dt.float32, mybir.dt.uint16
 ADD, MAX = mybir.AluOpType.add, mybir.AluOpType.max
+RELU = mybir.ActivationFunctionType.Relu
 
 P = 128
 S, D = 1024, 128
@@ -71,6 +72,9 @@ def tile_cls_model_kernel(tc, table, w, b, offs, out):
                 op=MAX,
             )
             pooled = work.tile([P, R], F32, name="pooled")
-            nc.vector.tensor_scalar(pooled[:], peak[:], bias[:, k : k + 1], 0.0, op0=ADD, op1=MAX)
+            if k < FEATURE_BLOCKS - 1:
+                nc.scalar.activation(pooled[:], peak[:], RELU, bias=bias[:, k : k + 1])
+            else:
+                nc.vector.tensor_scalar(pooled[:], peak[:], bias[:, k : k + 1], 0.0, op0=ADD, op1=MAX)
             queue = nc.sync if k % 2 == 0 else nc.scalar
             queue.dma_start(out[k * P : (k + 1) * P, :], pooled[:])

@@ -25,12 +25,13 @@ def tile_cls_model_kernel(tc, table, w, b, offs, out):
         tc.psum_pool(name="flip", bufs=CHUNKS) as flip,
         tc.psum_pool(name="prod", bufs=FEATURE_BLOCKS) as prod,
     ):
-        chunked = table.rearrange("(c p e) d -> c p e d", p=P, e=CHUNK // P)
+        neighbours = table.rearrange("(c p e) d -> c p e d", p=P, e=CHUNK // P)
+        halves = table.rearrange("(c e p) d -> c p e d", p=P, e=CHUNK // P)
         rows = []
         for c in range(CHUNKS):
             rows.append(held.tile([P, CHUNK // P, D], BF16, name=f"rows{c}"))
             queue = nc.sync if c % 2 == 0 else nc.scalar
-            queue.dma_start(rows[c][:], chunked[c])
+            queue.dma_start(rows[c][:], neighbours[c] if c < CHUNKS - 1 else halves[c])
 
         offsets = held.tile([P, N // 16], U16, name="offsets")
         nc.sync.dma_start(offsets[:], offs)
@@ -46,7 +47,7 @@ def tile_cls_model_kernel(tc, table, w, b, offs, out):
         make_identity(nc, identity[:])
 
         points = held.tile([D, S], BF16, name="points")
-        for c in range(CHUNKS):
+        for c in range(CHUNKS - 1):
             flipped = flip.tile([D, CHUNK], BF16, name="flipped")
             for e in range(CHUNK // P):
                 nc.tensor.transpose(flipped[:, e * P : (e + 1) * P], rows[c][:, e, :], identity[:])
@@ -54,6 +55,11 @@ def tile_cls_model_kernel(tc, table, w, b, offs, out):
                 points[:, c * CHUNK : (c + 1) * CHUNK].rearrange("d (p e) -> d p e", p=P),
                 flipped[:].rearrange("d (e p) -> d p e", p=P),
             )
+        for e in range(CHUNK // P):
+            flipped = flip.tile([D, CHUNK], BF16, name="flipped")
+            nc.tensor.transpose(flipped[:, :P], rows[CHUNKS - 1][:, e, :], identity[:])
+            first = (CHUNKS - 1) * CHUNK + e * P
+            nc.vector.tensor_copy(points[:, first : first + P], flipped[:, :P])
 
         for k in range(FEATURE_BLOCKS):
             product = prod.tile([P, N], F32, name="product")

@@ -40,8 +40,9 @@ def tile_cls_model_kernel(tc, table, w, b, offs, out):
         nc.sync.dma_start(weights[:], w)
 
         bias = held.tile([P, FEATURE_BLOCKS], F32, name="bias")
-        with nc.allow_non_contiguous_dma(reason="one float32 of the bias to a partition"):
-            nc.scalar.dma_start(bias[:], b.rearrange("(k p) one -> p (k one)", p=P))
+        nc.scalar.dma_start(bias[:], b.rearrange("(p k) one -> p (k one)", p=P))
+        block_weights = weights[:].rearrange("d (p k) -> d k p", p=P)
+        block_out = out.rearrange("(p k) r -> p k r", p=P)
 
         identity = held.tile([P, P], BF16, name="identity")
         make_identity(nc, identity[:])
@@ -65,7 +66,7 @@ def tile_cls_model_kernel(tc, table, w, b, offs, out):
             product = prod.tile([P, N], F32, name="product")
             nc.tensor.matmul(
                 product[:],
-                weights[:, k * P : (k + 1) * P],
+                block_weights[:, k, :],
                 points[:].indirect(offsets[:]),
                 start=True,
                 stop=True,
@@ -83,4 +84,4 @@ def tile_cls_model_kernel(tc, table, w, b, offs, out):
             else:
                 nc.vector.tensor_scalar(pooled[:], peak[:], bias[:, k : k + 1], 0.0, op0=ADD, op1=MAX)
             queue = nc.sync if k % 2 == 0 else nc.scalar
-            queue.dma_start(out[k * P : (k + 1) * P, :], pooled[:])
+            queue.dma_start(block_out[:, k, :], pooled[:])

@@ -47,6 +47,9 @@ def tile_cls_model_kernel(tc, table, w, b, offs, out):
         identity = held.tile([P, P], BF16, name="identity")
         make_identity(nc, identity[:])
 
+        table_call = held.tile([P, 1], F32, name="table_call")
+        nc.scalar.activation(table_call[:], identity[:, :1], RELU)
+
         points = held.tile([D, S], BF16, name="points")
         for c in range(CHUNKS - 1):
             flipped = flip.tile([D, CHUNK], BF16, name="flipped")

@@ -36,13 +36,14 @@ def tile_cls_model_kernel(tc, table, w, b, offs, out):
         offsets = held.tile([P, N // 16], U16, name="offsets")
         nc.sync.dma_start(offsets[:], offs)
 
-        weights = held.tile([D, M], BF16, name="weights")
-        nc.sync.dma_start(weights[:], w)
+        weights = []
+        for half, queue in enumerate((nc.sync, nc.scalar)):
+            weights.append(held.tile([D, M // 2], BF16, name=f"weights{half}"))
+            queue.dma_start(weights[half][:], w[:, half * M // 2 : (half + 1) * M // 2])
 
-        bias = held.tile([P, FEATURE_BLOCKS], F32, name="bias")
-        nc.scalar.dma_start(bias[:], b.rearrange("(p k) one -> p (k one)", p=P))
-        block_weights = weights[:].rearrange("d (p k) -> d k p", p=P)
-        block_out = out.rearrange("(p k) r -> p k r", p=P)
+        bias = held.tile([P, 2, 2], F32, name="bias")
+        nc.scalar.dma_start(bias[:], b.rearrange("(half p i) one -> p half (i one)", half=2, p=P))
+        block_out = out.rearrange("(half p i) r -> half p i r", half=2, p=P)
 
         identity = held.tile([P, P], BF16, name="identity")
         make_identity(nc, identity[:])
@@ -66,10 +67,11 @@ def tile_cls_model_kernel(tc, table, w, b, offs, out):
             nc.vector.tensor_copy(points[:, first : first + P], flipped[:, :P])
 
         for k in range(FEATURE_BLOCKS):
+            half, i = divmod(k, 2)
             product = prod.tile([P, N], F32, name="product")
             nc.tensor.matmul(
                 product[:],
-                block_weights[:, k, :],
+                weights[half][:].rearrange("d (p i) -> d i p", p=P)[:, i, :],
                 points[:].indirect(offsets[:]),
                 start=True,
                 stop=True,
@@ -83,8 +85,8 @@ def tile_cls_model_kernel(tc, table, w, b, offs, out):
             )
             pooled = work.tile([P, R], F32, name="pooled")
             if k < FEATURE_BLOCKS - 1:
-                nc.scalar.activation(pooled[:], peak[:], RELU, bias=bias[:, k : k + 1])
+                nc.scalar.activation(pooled[:], peak[:], RELU, bias=bias[:, half, i : i + 1])
             else:
-                nc.vector.tensor_scalar(pooled[:], peak[:], bias[:, k : k + 1], 0.0, op0=ADD, op1=MAX)
+                nc.vector.tensor_scalar(pooled[:], peak[:], bias[:, half, i : i + 1], 0.0, op0=ADD, op1=MAX)
             queue = nc.sync if k % 2 == 0 else nc.scalar
-            queue.dma_start(block_out[:, k, :], pooled[:])
+            queue.dma_start(block_out[half, :, i, :], pooled[:])

import concourse.mybir as mybir
from concourse.masks import make_identity

BF16, F32, U16 = mybir.dt.bfloat16, mybir.dt.float32, mybir.dt.uint16
ADD, MAX = mybir.AluOpType.add, mybir.AluOpType.max
RELU = mybir.ActivationFunctionType.Relu

P = 128
S, D = 1024, 128
M = 512
N, Q = 256, 4
R = N // Q
CHUNK = 2 * P
CHUNKS = S // CHUNK
FEATURE_BLOCKS = M // P

FLOPS = 2 * D * M * N


def tile_cls_model_kernel(tc, table, w, b, offs, out):
    nc = tc.nc
    with (
        tc.tile_pool(name="held", bufs=1) as held,
        tc.tile_pool(name="work", bufs=FEATURE_BLOCKS) as work,
        tc.psum_pool(name="flip", bufs=CHUNKS) as flip,
        tc.psum_pool(name="prod", bufs=FEATURE_BLOCKS) as prod,
    ):
        neighbours = table.rearrange("(c p e) d -> c p e d", p=P, e=CHUNK // P)
        halves = table.rearrange("(c e p) d -> c p e d", p=P, e=CHUNK // P)
        rows = []
        for c in range(CHUNKS):
            rows.append(held.tile([P, CHUNK // P, D], BF16, name=f"rows{c}"))
            queue = nc.sync if c % 2 == 0 else nc.scalar
            queue.dma_start(rows[c][:], neighbours[c] if c < CHUNKS - 1 else halves[c])

        offsets = held.tile([P, N // 16], U16, name="offsets")
        nc.sync.dma_start(offsets[:], offs)

        weights = []
        for half, queue in enumerate((nc.sync, nc.scalar)):
            weights.append(held.tile([D, M // 2], BF16, name=f"weights{half}"))
            queue.dma_start(weights[half][:], w[:, half * M // 2 : (half + 1) * M // 2])

        bias = held.tile([P, 2, 2], F32, name="bias")
        nc.scalar.dma_start(bias[:], b.rearrange("(half p i) one -> p half (i one)", half=2, p=P))
        block_out = out.rearrange("(half p i) r -> half p i r", half=2, p=P)

        identity = held.tile([P, P], BF16, name="identity")
        make_identity(nc, identity[:])

        table_call = held.tile([P, 1], F32, name="table_call")
        nc.scalar.activation(table_call[:], identity[:, :1], RELU)

        points = held.tile([D, S], BF16, name="points")
        for c in range(CHUNKS - 1):
            flipped = flip.tile([D, CHUNK], BF16, name="flipped")
            for e in range(CHUNK // P):
                nc.tensor.transpose(flipped[:, e * P : (e + 1) * P], rows[c][:, e, :], identity[:])
            nc.vector.tensor_copy(
                points[:, c * CHUNK : (c + 1) * CHUNK].rearrange("d (p e) -> d p e", p=P),
                flipped[:].rearrange("d (e p) -> d p e", p=P),
            )
        for e in range(CHUNK // P):
            flipped = flip.tile([D, CHUNK], BF16, name="flipped")
            nc.tensor.transpose(flipped[:, :P], rows[CHUNKS - 1][:, e, :], identity[:])
            first = (CHUNKS - 1) * CHUNK + e * P
            nc.vector.tensor_copy(points[:, first : first + P], flipped[:, :P])

        for k in range(FEATURE_BLOCKS):
            half, i = divmod(k, 2)
            product = prod.tile([P, N], F32, name="product")
            nc.tensor.matmul(
                product[:],
                weights[half][:].rearrange("d (p i) -> d i p", p=P)[:, i, :],
                points[:].indirect(offsets[:]),
                start=True,
                stop=True,
            )
            peak = work.tile([P, R], F32, name="peak")
            nc.vector.tensor_reduce(
                out=peak[:],
                in_=product[:].rearrange("p (r q) -> p r q", q=Q),
                axis=mybir.AxisListType.X,
                op=MAX,
            )
            pooled = work.tile([P, R], F32, name="pooled")
            if k < FEATURE_BLOCKS - 1:
                nc.scalar.activation(pooled[:], peak[:], RELU, bias=bias[:, half, i : i + 1])
            else:
                nc.vector.tensor_scalar(pooled[:], peak[:], bias[:, half, i : i + 1], 0.0, op0=ADD, op1=MAX)
            queue = nc.sync if k % 2 == 0 else nc.scalar
            queue.dma_start(block_out[half, :, i, :], pooled[:])
